import numpy as np
import ml_dtypes


def mxq(x, axis, fmt="e4m3"):
    dtype, down = {"e4m3": (ml_dtypes.float8_e4m3fn, 7), "e5m2": (ml_dtypes.float8_e5m2, 14)}[fmt]
    v = np.moveaxis(np.asarray(x, np.float32).astype(ml_dtypes.bfloat16).astype(np.float64), axis, -1)
    blocks = v.reshape(v.shape[:-1] + (-1, 32))
    amax = np.abs(blocks).max(-1, keepdims=True)
    byte = np.maximum(np.where(amax > 0, np.frexp(amax)[1] - 1 + 127, 0) - down, 1)
    scale = np.exp2(byte - 127.0)
    codes = (blocks / scale).astype(np.float32).astype(dtype).astype(np.float64)
    return np.moveaxis((codes * scale).reshape(v.shape), -1, axis)


WIDE = False


def mx_kscale(k):
    if not WIDE:
        return np.ones(k)
    levels = np.array([30, -30])
    if k % 512:
        return np.exp2(np.random.permutation(np.resize(levels, k // 32))).repeat(32)
    a = np.empty((k // 512, 16))
    for p in range(k // 512):
        a[p, :8] = np.random.permutation(np.resize(levels, 8))
        for g in range(8):
            far = levels[np.abs(levels - a[p, g]) >= 10]
            a[p, g + 8] = far[np.random.randint(len(far))]
    return np.exp2(a.ravel()).repeat(32)


BF16 = ml_dtypes.bfloat16


def bf(x):
    return np.asarray(x, np.float32).astype(BF16)


def f64(x):
    return np.asarray(x).astype(np.float64)


I, H, B = 2048, 2048, 128


def sigmoid(v):
    return 1.0 / (1.0 + np.exp(-v))


def setup_inputs():
    s, t = mx_kscale(I), mx_kscale(H)
    d = {"x": bf(np.random.standard_normal((I, B)) * s[:, None]), "h": bf(np.random.standard_normal((B, H)) * t[None, :]),
         "c": bf(np.random.standard_normal((B, H))), "ig": bf(np.random.standard_normal((H, B)) * 0.35)}
    for n in ("w_if", "w_io"):
        d[n] = bf(np.random.standard_normal((H, I)) * 0.7 / np.sqrt(I) / s[None, :])
    for n in ("w_hf", "w_ho"):
        d[n] = bf(np.random.standard_normal((H, H)) * 0.7 / np.sqrt(H) / t[None, :])
    for n in ("b_if", "b_hf", "b_io", "b_ho"):
        d[n] = bf(np.random.standard_normal((H, 1)) * 0.3)
    return d


def reference(x, h, c, ig, w_if, w_io, w_hf, w_ho, b_if, b_hf, b_io, b_ho):
    xq = mxq(f64(x), 0, "e4m3")
    hq = mxq(f64(h).T, 0, "e4m3")
    f = sigmoid((mxq(f64(w_if), 1, "e5m2") @ xq) + f64(b_if) + (mxq(f64(w_hf), 1, "e5m2") @ hq) + f64(b_hf))
    o = sigmoid((mxq(f64(w_io), 1, "e5m2") @ xq) + f64(b_io) + (mxq(f64(w_ho), 1, "e5m2") @ hq) + f64(b_ho))
    c_next_t = f * f64(c).T + f64(ig)
    h_next_t = o * np.tanh(c_next_t)
    return h_next_t.T, c_next_t.T

@@ -1,0 +1,266 @@
+from contextlib import ExitStack
+
+import concourse.mybir as mybir
+from concourse.masks import make_identity
+
+I, H, B = 2048, 2048, 128
+FLOPS = 4 * 2 * B * H * I
+
+F32 = mybir.dt.float32
+BF16 = mybir.dt.bfloat16
+U32 = mybir.dt.uint32
+U8 = mybir.dt.uint8
+E4M3 = mybir.dt.float8_e4m3fn_x4
+E5M2 = mybir.dt.float8_e5m2_x4
+ACT = mybir.ActivationFunctionType
+ALU = mybir.AluOpType
+
+P = 128
+PASSES = I // 512
+ROWS = 256
+BLOCKS = H // ROWS
+STEPS = 4 * BLOCKS
+DIRECT = 1
+LEAD = 5
+HEAD_BIAS = 4
+
+
+def tile_naivelstm_pb_kernel(tc, x, h, c, ig, w_if, w_io, w_hf, w_ho, b_if, b_hf, b_io, b_ho, out_0, out_1):
+    nc = tc.nc
+    weights = [w_if, w_hf, w_io, w_ho]
+
+    with ExitStack() as ctx:
+        keep = ctx.enter_context(tc.tile_pool(name="keep", bufs=1))
+        raw_pool = ctx.enter_context(tc.tile_pool(name="raw", bufs=LEAD + 2))
+        split_pool = ctx.enter_context(tc.tile_pool(name="split", bufs=3))
+        group_pool = ctx.enter_context(tc.tile_pool(name="group", bufs=5))
+        code_pool = ctx.enter_context(tc.tile_pool(name="code", bufs=6))
+        gate_pool = ctx.enter_context(tc.tile_pool(name="gate", bufs=3))
+        turn_psum = ctx.enter_context(tc.psum_pool(name="turn", bufs=5))
+        acc_psum = ctx.enter_context(tc.psum_pool(name="acc", bufs=1))
+        ctx.enter_context(tc.manual_schedule())
+
+        ident16 = keep.tile([P, P], BF16, name="ident16")
+        ident32 = keep.tile([P, P], F32, name="ident32")
+        bias_rows = keep.tile([P, ROWS], BF16, name="bias_rows")
+        pick = keep.tile([P, 2 * BLOCKS], BF16, name="pick")
+        bias = keep.tile([P, BLOCKS, 2 * ROWS], F32, name="bias")
+        x_raw = keep.tile([P, PASSES, 4 * B], BF16, name="x_raw")
+        h_raw = keep.tile([P, H], BF16, name="h_raw")
+        x_grouped = keep.tile([P, PASSES * 4 * B], BF16, name="x_grouped", align_bytes=64)
+        h_grouped = keep.tile([P, PASSES * 4 * B], BF16, name="h_grouped", align_bytes=64)
+        x_codes = keep.tile([P, PASSES * B], U32, name="x_codes", align_bytes=64)
+        h_codes = keep.tile([P, PASSES * B], U32, name="h_codes", align_bytes=64)
+        x_scales = keep.tile([P, PASSES * B], U8, name="x_scales", align_bytes=64)
+        h_scales = keep.tile([P, PASSES * B], U8, name="h_scales", align_bytes=64)
+
+        raw, split, grouped, quantised, live = {}, {}, {}, {}, {}
+
+        def direct_passes(s):
+            return PASSES if s in (0, STEPS - 1) else DIRECT
+
+        def load_weights(s):
+            block, which = divmod(s, 4)
+            raw[s] = raw_pool.tile([P, 2 * I], BF16, name="w_raw", tag="w_raw")
+            rows = weights[which][block * ROWS : (block + 1) * ROWS, :]
+            nc.sync.dma_start(out=raw[s][:], in_=rows.rearrange("(p j) k -> p (j k)", j=2))
+
+        def load_state(pair):
+            cols = slice(pair * 2 * ROWS, (pair + 1) * 2 * ROWS)
+            live["c", pair] = gate_pool.tile([P, 2 * ROWS], BF16, name="c_in", tag="c_in")
+            nc.sync.dma_start(out=live["c", pair][:], in_=c[:, cols])
+            live["ig", pair] = gate_pool.tile([P, 4 * B], BF16, name="ig_in", tag="ig_in")
+            nc.sync.dma_start(out=live["ig", pair][:], in_=ig[cols, :].rearrange("(p j) b -> p (j b)", j=4))
+
+        def split_words(s):
+            split[s] = split_pool.tile([P, 2, 2, (PASSES - DIRECT) * P], F32, name="w_split", tag="w_split")
+            words = raw[s][:].bitcast(F32).rearrange("p (j w u) -> p j u w", j=2, u=2)
+            nc.vector.tensor_copy(out=split[s][:], in_=words[:, :, :, DIRECT * P :])
+
+        def turn_weights(s):
+            words = raw[s][:].bitcast(F32)
+            for g in range(PASSES):
+                bank = turn_psum.tile([P, 4, P], F32, name="turned", tag="turned")
+                for j in range(2):
+                    for u in range(2):
+                        if g < direct_passes(s):
+                            first = j * (I // 2) + g * 2 * P
+                            source = words[:, first + u : first + 2 * P : 2]
+                        else:
+                            source = split[s][:, j, u, (g - DIRECT) * P : (g - DIRECT + 1) * P]
+                        nc.tensor.transpose(bank[:, 2 * j + u, :], source, ident32[:])
+                half, gl = divmod(g, 2)
+                if gl == 0:
+                    grouped[s, half] = group_pool.tile([P, 2, 4 * ROWS], BF16, name="w_grouped", tag="w_grouped", align_bytes=64)
+                nc.scalar.copy(
+                    out=grouped[s, half][:, gl, :].bitcast(F32).rearrange("p (r q) -> p r q", q=4),
+                    in_=bank[:].rearrange("p q r -> p r q"),
+                )
+
+        def quantise_weights(s, half):
+            codes = code_pool.tile([P, 2 * ROWS], U32, name="w_codes", tag="w_codes", align_bytes=64)
+            scales = code_pool.tile([P, 2 * ROWS], U8, name="w_scales", tag="w_scales", align_bytes=64)
+            nc.vector.quantize_mx(
+                out=codes[:].bitcast(E5M2), scales=scales[:], in_=grouped[s, half][:].rearrange("p g n -> p (g n)")
+            )
+            quantised[s, half] = (codes, scales)
+
+        def multiply(s):
+            block, which = divmod(s, 4)
+            gate, recurrent = divmod(which, 2)
+            if not recurrent:
+                live["acc", gate] = acc_psum.tile([P, ROWS], F32, name="acc%d" % gate, tag="acc%d" % gate)
+            a_codes, a_scales = (h_codes, h_scales) if recurrent else (x_codes, x_scales)
+            for g in range(PASSES):
+                half, gl = divmod(g, 2)
+                codes, scales = quantised[s, half]
+                nc.tensor.matmul_mx(
+                    out=live["acc", gate][:],
+                    lhsT=a_codes[:, g * B : (g + 1) * B].bitcast(E4M3),
+                    lhsT_scale=a_scales[:, g * B : (g + 1) * B],
+                    rhs=codes[:, gl * ROWS : (gl + 1) * ROWS].bitcast(E5M2),
+                    rhs_scale=scales[:, gl * ROWS : (gl + 1) * ROWS],
+                    start=(not recurrent and g == 0),
+                    stop=(recurrent == 1 and g == PASSES - 1),
+                )
+
+        def spread_bias(block):
+            bank = turn_psum.tile([P, 2 * ROWS], F32, name="spread", tag="turned")
+            for gate in range(2):
+                m = gate * BLOCKS + block
+                nc.tensor.matmul(
+                    bank[:, gate * ROWS : (gate + 1) * ROWS],
+                    lhsT=pick[:, m : m + 1].to_broadcast([P, P]),
+                    rhs=bias_rows[:],
+                    start=True,
+                    stop=True,
+                )
+            nc.vector.tensor_copy(out=bias[:, block, :], in_=bank[:])
+
+        def turn_ig(pair):
+            live["igT", pair] = acc_psum.tile([P, 4, P], BF16, name="ig_turned", tag="ig_turned")
+            for j in range(4):
+                nc.tensor.transpose(live["igT", pair][:, j, :], live["ig", pair][:, j * B : (j + 1) * B], ident16[:])
+
+        def turn_h():
+            words = h_raw[:].bitcast(F32)
+            for half in range(2):
+                bank = turn_psum.tile([P, 2, 2, P], F32, name="h_turned", tag="turned")
+                for gl in range(2):
+                    first = (2 * half + gl) * 2 * P
+                    for u in range(2):
+                        nc.tensor.transpose(bank[:, gl, u, :], words[:, first + u : first + 2 * P : 2], ident32[:])
+                target = h_grouped[:, half * 8 * B : (half + 1) * 8 * B].bitcast(F32)
+                nc.vector.tensor_copy(
+                    out=target.rearrange("p (g b u) -> p g b u", g=2, u=2), in_=bank[:].rearrange("p g u b -> p g b u")
+                )
+
+        def add_bias(block, gate):
+            live["z", gate] = gate_pool.tile([P, ROWS], F32, name="z", tag="z")
+            nc.vector.tensor_tensor(
+                out=live["z", gate][:], in0=live["acc", gate][:], in1=bias[:, block, gate * ROWS : (gate + 1) * ROWS], op=ALU.add
+            )
+
+        def squash(source, target, func):
+            live[target] = gate_pool.tile([P, ROWS], F32, name=target, tag=target)
+            nc.scalar.activation(out=live[target][:], in_=live[source][:], func=func)
+
+        def forget(block):
+            pair, a = divmod(block, 2)
+            live["kept"] = gate_pool.tile([P, ROWS], F32, name="kept", tag="kept")
+            nc.vector.tensor_tensor(
+                out=live["kept"][:], in0=live["f"][:], in1=live["c", pair][:, a * ROWS : (a + 1) * ROWS], op=ALU.mult
+            )
+
+        def update_cell(block):
+            pair, a = divmod(block, 2)
+            live["c_next"] = gate_pool.tile([P, ROWS], F32, name="c_next", tag="c_next")
+            nc.vector.tensor_tensor(
+                out=live["c_next"][:].rearrange("b (r j) -> b r j", j=4),
+                in0=live["kept"][:].rearrange("b (r j) -> b r j", j=4),
+                in1=live["igT", pair][:].rearrange("b j r -> b r j")[:, a * (ROWS // 4) : (a + 1) * (ROWS // 4), :],
+                op=ALU.add,
+            )
+
+        def update_hidden():
+            live["h_next"] = gate_pool.tile([P, ROWS], F32, name="h_next", tag="h_next")
+            nc.vector.tensor_tensor(out=live["h_next"][:], in0=live["o"][:], in1=live["tanh_c"][:], op=ALU.mult)
+
+        def store(name, out, block):
+            nc.sync.dma_start(out=out[:, block * ROWS : (block + 1) * ROWS], in_=live[name][:])
+
+        for n, b in enumerate((b_if, b_io, b_hf, b_ho)):
+            nc.scalar.dma_start(
+                out=bias_rows[n * BLOCKS : (n + 1) * BLOCKS, :], in_=b.rearrange("(r n) o -> r (n o)", r=BLOCKS)
+            )
+        load_weights(0)
+        nc.sync.dma_start(out=x_raw[:], in_=x.rearrange("(g p j) b -> p g (j b)", g=PASSES, j=4))
+        load_weights(1)
+        nc.sync.dma_start(out=h_raw[:], in_=h)
+        load_weights(2)
+        load_state(0)
+        for s in range(3, LEAD):
+            load_weights(s)
+        make_identity(nc, ident16[:])
+        make_identity(nc, ident32[:])
+        nc.vector.memset(bias_rows[32:64, :], 0.0)
+        nc.vector.memset(bias_rows[64:128, :], 0.0)
+        nc.vector.tensor_tensor(
+            out=pick[:], in0=ident16[:, 0 : 2 * BLOCKS], in1=ident16[:, 2 * BLOCKS : 4 * BLOCKS], op=ALU.add
+        )
+        for block in range(HEAD_BIAS):
+            spread_bias(block)
+
+        for s in range(STEPS + 4):
+            block, phase = divmod(s - 3, 4)
+            ending = 0 <= block < BLOCKS
+            if s + LEAD < STEPS:
+                load_weights(s + LEAD)
+            if s % 8 == 4 and s // 8 + 1 < BLOCKS // 2:
+                load_state(s // 8 + 1)
+            if ending and phase == 3:
+                store("c_next", out_1, block)
+            if block >= 1 and phase == 0:
+                store("h_next", out_0, block - 1)
+
+            if s == 2:
+                turn_h()
+            if ending and phase == 0 and block % 2 == 0:
+                turn_ig(block // 2)
+            if s < STEPS:
+                turn_weights(s)
+
+            if s == 0:
+                nc.vector.tensor_copy(
+                    out=x_grouped[:].rearrange("p (g b j) -> p g b j", g=PASSES, j=4),
+                    in_=x_raw[:].rearrange("p g (j b) -> p g b j", j=4),
+                )
+            if 1 <= s <= STEPS:
+                quantise_weights(s - 1, 0)
+            if ending and phase == 2:
+                update_cell(block)
+            if s + 1 < STEPS and direct_passes(s + 1) < PASSES:
+                split_words(s + 1)
+            if 1 <= s <= STEPS:
+                quantise_weights(s - 1, 1)
+            if s == 0:
+                nc.vector.quantize_mx(out=x_codes[:].bitcast(E4M3), scales=x_scales[:], in_=x_grouped[:])
+            if s == 2:
+                nc.vector.quantize_mx(out=h_codes[:].bitcast(E4M3), scales=h_scales[:], in_=h_grouped[:])
+
+            if ending and phase == 3 and block + HEAD_BIAS < BLOCKS:
+                spread_bias(block + HEAD_BIAS)
+            if 2 <= s < STEPS + 2:
+                multiply(s - 2)
+
+            if ending and phase == 0:
+                add_bias(block, 0)
+                squash(("z", 0), "f", ACT.Sigmoid)
+            if ending and phase == 1:
+                forget(block)
+            if ending and phase == 2:
+                add_bias(block, 1)
+                squash("c_next", "tanh_c", ACT.Tanh)
+                squash(("z", 1), "o", ACT.Sigmoid)
+            if ending and phase == 3:
+                update_hidden()

@@ -20,9 +20,8 @@ PASSES = I // 512
 ROWS = 256
 BLOCKS = H // ROWS
 STEPS = 4 * BLOCKS
-DIRECT = 1
+DIRECT = 2
 LEAD = 5
-HEAD_BIAS = 4
 
 
 def tile_naivelstm_pb_kernel(tc, x, h, c, ig, w_if, w_io, w_hf, w_ho, b_if, b_hf, b_io, b_ho, out_0, out_1):
@@ -77,6 +76,16 @@ def tile_naivelstm_pb_kernel(tc, x, h, c, ig, w_if, w_io, w_hf, w_ho, b_if, b_hf
             words = raw[s][:].bitcast(F32).rearrange("p (j w u) -> p j u w", j=2, u=2)
             nc.vector.tensor_copy(out=split[s][:], in_=words[:, :, :, DIRECT * P :])
 
+        def vector_helps(s):
+            return s % 4 == 3
+
+        def group_words(copy, s, g):
+            half, gl = divmod(g, 2)
+            copy(
+                out=grouped[s, half][:, gl, :].bitcast(F32).rearrange("p (r q) -> p r q", q=4),
+                in_=live["turned", g][:].rearrange("p q r -> p r q"),
+            )
+
         def turn_weights(s):
             words = raw[s][:].bitcast(F32)
             for g in range(PASSES):
@@ -92,10 +101,9 @@ def tile_naivelstm_pb_kernel(tc, x, h, c, ig, w_if, w_io, w_hf, w_ho, b_if, b_hf
                 half, gl = divmod(g, 2)
                 if gl == 0:
                     grouped[s, half] = group_pool.tile([P, 2, 4 * ROWS], BF16, name="w_grouped", tag="w_grouped", align_bytes=64)
-                nc.scalar.copy(
-                    out=grouped[s, half][:, gl, :].bitcast(F32).rearrange("p (r q) -> p r q", q=4),
-                    in_=bank[:].rearrange("p q r -> p r q"),
-                )
+                live["turned", g] = bank
+                if g < PASSES - 1 or not vector_helps(s):
+                    group_words(nc.scalar.copy, s, g)
 
         def quantise_weights(s, half):
             codes = code_pool.tile([P, 2 * ROWS], U32, name="w_codes", tag="w_codes", align_bytes=64)
@@ -124,7 +132,7 @@ def tile_naivelstm_pb_kernel(tc, x, h, c, ig, w_if, w_io, w_hf, w_ho, b_if, b_hf
                     stop=(recurrent == 1 and g == PASSES - 1),
                 )
 
-        def spread_bias(block):
+        def spread_bias(block, copy):
             bank = turn_psum.tile([P, 2 * ROWS], F32, name="spread", tag="turned")
             for gate in range(2):
                 m = gate * BLOCKS + block
@@ -135,7 +143,7 @@ def tile_naivelstm_pb_kernel(tc, x, h, c, ig, w_if, w_io, w_hf, w_ho, b_if, b_hf
                     start=True,
                     stop=True,
                 )
-            nc.vector.tensor_copy(out=bias[:, block, :], in_=bank[:])
+            copy(out=bias[:, block, :], in_=bank[:])
 
         def turn_ig(pair):
             live["igT", pair] = acc_psum.tile([P, 4, P], BF16, name="ig_turned", tag="ig_turned")
@@ -151,7 +159,7 @@ def tile_naivelstm_pb_kernel(tc, x, h, c, ig, w_if, w_io, w_hf, w_ho, b_if, b_hf
                     for u in range(2):
                         nc.tensor.transpose(bank[:, gl, u, :], words[:, first + u : first + 2 * P : 2], ident32[:])
                 target = h_grouped[:, half * 8 * B : (half + 1) * 8 * B].bitcast(F32)
-                nc.vector.tensor_copy(
+                nc.scalar.copy(
                     out=target.rearrange("p (g b u) -> p g b u", g=2, u=2), in_=bank[:].rearrange("p g u b -> p g b u")
                 )
 
@@ -194,22 +202,21 @@ def tile_naivelstm_pb_kernel(tc, x, h, c, ig, w_if, w_io, w_hf, w_ho, b_if, b_hf
                 out=bias_rows[n * BLOCKS : (n + 1) * BLOCKS, :], in_=b.rearrange("(r n) o -> r (n o)", r=BLOCKS)
             )
         load_weights(0)
-        nc.sync.dma_start(out=x_raw[:], in_=x.rearrange("(g p j) b -> p g (j b)", g=PASSES, j=4))
         load_weights(1)
-        nc.sync.dma_start(out=h_raw[:], in_=h)
+        nc.sync.dma_start(out=x_raw[:], in_=x.rearrange("(g p j) b -> p g (j b)", g=PASSES, j=4))
         load_weights(2)
+        nc.sync.dma_start(out=h_raw[:], in_=h)
+        load_weights(3)
         load_state(0)
-        for s in range(3, LEAD):
+        for s in range(4, LEAD):
             load_weights(s)
-        make_identity(nc, ident16[:])
         make_identity(nc, ident32[:])
+        make_identity(nc, ident16[:])
         nc.vector.memset(bias_rows[32:64, :], 0.0)
         nc.vector.memset(bias_rows[64:128, :], 0.0)
         nc.vector.tensor_tensor(
             out=pick[:], in0=ident16[:, 0 : 2 * BLOCKS], in1=ident16[:, 2 * BLOCKS : 4 * BLOCKS], op=ALU.add
         )
-        for block in range(HEAD_BIAS):
-            spread_bias(block)
 
         for s in range(STEPS + 4):
             block, phase = divmod(s - 3, 4)
@@ -223,18 +230,15 @@ def tile_naivelstm_pb_kernel(tc, x, h, c, ig, w_if, w_io, w_hf, w_ho, b_if, b_hf
             if block >= 1 and phase == 0:
                 store("h_next", out_0, block - 1)
 
-            if s == 2:
-                turn_h()
-            if ending and phase == 0 and block % 2 == 0:
+            if ending and phase == 1 and block % 2 == 0:
                 turn_ig(block // 2)
             if s < STEPS:
                 turn_weights(s)
-
             if s == 0:
-                nc.vector.tensor_copy(
-                    out=x_grouped[:].rearrange("p (g b j) -> p g b j", g=PASSES, j=4),
-                    in_=x_raw[:].rearrange("p g (j b) -> p g b j", j=4),
-                )
+                spread_bias(0, lambda out, in_: nc.scalar.activation(out=out, in_=in_, func=ACT.Copy))
+            if s == 2:
+                turn_h()
+
             if 1 <= s <= STEPS:
                 quantise_weights(s - 1, 0)
             if ending and phase == 2:
@@ -243,13 +247,20 @@ def tile_naivelstm_pb_kernel(tc, x, h, c, ig, w_if, w_io, w_hf, w_ho, b_if, b_hf
                 split_words(s + 1)
             if 1 <= s <= STEPS:
                 quantise_weights(s - 1, 1)
+            if s < STEPS and vector_helps(s):
+                group_words(nc.vector.tensor_copy, s, PASSES - 1)
             if s == 0:
+                nc.vector.tensor_copy(
+                    out=x_grouped[:].rearrange("p (g b j) -> p g b j", g=PASSES, j=4),
+                    in_=x_raw[:].rearrange("p g (j b) -> p g b j", j=4),
+                )
+            if s == 1:
                 nc.vector.quantize_mx(out=x_codes[:].bitcast(E4M3), scales=x_scales[:], in_=x_grouped[:])
             if s == 2:
                 nc.vector.quantize_mx(out=h_codes[:].bitcast(E4M3), scales=h_scales[:], in_=h_grouped[:])
 
-            if ending and phase == 3 and block + HEAD_BIAS < BLOCKS:
-                spread_bias(block + HEAD_BIAS)
+            if ending and phase == 3 and block + 1 < BLOCKS:
+                spread_bias(block + 1, nc.vector.tensor_copy)
             if 2 <= s < STEPS + 2:
                 multiply(s - 2)
 

from contextlib import ExitStack

import concourse.mybir as mybir
from concourse.masks import make_identity

I, H, B = 2048, 2048, 128
FLOPS = 4 * 2 * B * H * I

F32 = mybir.dt.float32
BF16 = mybir.dt.bfloat16
U32 = mybir.dt.uint32
U8 = mybir.dt.uint8
E4M3 = mybir.dt.float8_e4m3fn_x4
E5M2 = mybir.dt.float8_e5m2_x4
ACT = mybir.ActivationFunctionType
ALU = mybir.AluOpType

P = 128
PASSES = I // 512
ROWS = 256
BLOCKS = H // ROWS
STEPS = 4 * BLOCKS
DIRECT = 2
LEAD = 5


def tile_naivelstm_pb_kernel(tc, x, h, c, ig, w_if, w_io, w_hf, w_ho, b_if, b_hf, b_io, b_ho, out_0, out_1):
    nc = tc.nc
    weights = [w_if, w_hf, w_io, w_ho]

    with ExitStack() as ctx:
        keep = ctx.enter_context(tc.tile_pool(name="keep", bufs=1))
        raw_pool = ctx.enter_context(tc.tile_pool(name="raw", bufs=LEAD + 2))
        split_pool = ctx.enter_context(tc.tile_pool(name="split", bufs=3))
        group_pool = ctx.enter_context(tc.tile_pool(name="group", bufs=5))
        code_pool = ctx.enter_context(tc.tile_pool(name="code", bufs=6))
        gate_pool = ctx.enter_context(tc.tile_pool(name="gate", bufs=3))
        turn_psum = ctx.enter_context(tc.psum_pool(name="turn", bufs=5))
        acc_psum = ctx.enter_context(tc.psum_pool(name="acc", bufs=1))
        ctx.enter_context(tc.manual_schedule())

        ident16 = keep.tile([P, P], BF16, name="ident16")
        ident32 = keep.tile([P, P], F32, name="ident32")
        bias_rows = keep.tile([P, ROWS], BF16, name="bias_rows")
        pick = keep.tile([P, 2 * BLOCKS], BF16, name="pick")
        bias = keep.tile([P, BLOCKS, 2 * ROWS], F32, name="bias")
        x_raw = keep.tile([P, PASSES, 4 * B], BF16, name="x_raw")
        h_raw = keep.tile([P, H], BF16, name="h_raw")
        x_grouped = keep.tile([P, PASSES * 4 * B], BF16, name="x_grouped", align_bytes=64)
        h_grouped = keep.tile([P, PASSES * 4 * B], BF16, name="h_grouped", align_bytes=64)
        x_codes = keep.tile([P, PASSES * B], U32, name="x_codes", align_bytes=64)
        h_codes = keep.tile([P, PASSES * B], U32, name="h_codes", align_bytes=64)
        x_scales = keep.tile([P, PASSES * B], U8, name="x_scales", align_bytes=64)
        h_scales = keep.tile([P, PASSES * B], U8, name="h_scales", align_bytes=64)

        raw, split, grouped, quantised, live = {}, {}, {}, {}, {}

        def direct_passes(s):
            return PASSES if s in (0, STEPS - 1) else DIRECT

        def load_weights(s):
            block, which = divmod(s, 4)
            raw[s] = raw_pool.tile([P, 2 * I], BF16, name="w_raw", tag="w_raw")
            rows = weights[which][block * ROWS : (block + 1) * ROWS, :]
            nc.sync.dma_start(out=raw[s][:], in_=rows.rearrange("(p j) k -> p (j k)", j=2))

        def load_state(pair):
            cols = slice(pair * 2 * ROWS, (pair + 1) * 2 * ROWS)
            live["c", pair] = gate_pool.tile([P, 2 * ROWS], BF16, name="c_in", tag="c_in")
            nc.sync.dma_start(out=live["c", pair][:], in_=c[:, cols])
            live["ig", pair] = gate_pool.tile([P, 4 * B], BF16, name="ig_in", tag="ig_in")
            nc.sync.dma_start(out=live["ig", pair][:], in_=ig[cols, :].rearrange("(p j) b -> p (j b)", j=4))

        def split_words(s):
            split[s] = split_pool.tile([P, 2, 2, (PASSES - DIRECT) * P], F32, name="w_split", tag="w_split")
            words = raw[s][:].bitcast(F32).rearrange("p (j w u) -> p j u w", j=2, u=2)
            nc.vector.tensor_copy(out=split[s][:], in_=words[:, :, :, DIRECT * P :])

        def vector_helps(s):
            return s % 4 == 3

        def group_words(copy, s, g):
            half, gl = divmod(g, 2)
            copy(
                out=grouped[s, half][:, gl, :].bitcast(F32).rearrange("p (r q) -> p r q", q=4),
                in_=live["turned", g][:].rearrange("p q r -> p r q"),
            )

        def turn_weights(s):
            words = raw[s][:].bitcast(F32)
            for g in range(PASSES):
                bank = turn_psum.tile([P, 4, P], F32, name="turned", tag="turned")
                for j in range(2):
                    for u in range(2):
                        if g < direct_passes(s):
                            first = j * (I // 2) + g * 2 * P
                            source = words[:, first + u : first + 2 * P : 2]
                        else:
                            source = split[s][:, j, u, (g - DIRECT) * P : (g - DIRECT + 1) * P]
                        nc.tensor.transpose(bank[:, 2 * j + u, :], source, ident32[:])
                half, gl = divmod(g, 2)
                if gl == 0:
                    grouped[s, half] = group_pool.tile([P, 2, 4 * ROWS], BF16, name="w_grouped", tag="w_grouped", align_bytes=64)
                live["turned", g] = bank
                if g < PASSES - 1 or not vector_helps(s):
                    group_words(nc.scalar.copy, s, g)

        def quantise_weights(s, half):
            codes = code_pool.tile([P, 2 * ROWS], U32, name="w_codes", tag="w_codes", align_bytes=64)
            scales = code_pool.tile([P, 2 * ROWS], U8, name="w_scales", tag="w_scales", align_bytes=64)
            nc.vector.quantize_mx(
                out=codes[:].bitcast(E5M2), scales=scales[:], in_=grouped[s, half][:].rearrange("p g n -> p (g n)")
            )
            quantised[s, half] = (codes, scales)

        def multiply(s):
            block, which = divmod(s, 4)
            gate, recurrent = divmod(which, 2)
            if not recurrent:
                live["acc", gate] = acc_psum.tile([P, ROWS], F32, name="acc%d" % gate, tag="acc%d" % gate)
            a_codes, a_scales = (h_codes, h_scales) if recurrent else (x_codes, x_scales)
            for g in range(PASSES):
                half, gl = divmod(g, 2)
                codes, scales = quantised[s, half]
                nc.tensor.matmul_mx(
                    out=live["acc", gate][:],
                    lhsT=a_codes[:, g * B : (g + 1) * B].bitcast(E4M3),
                    lhsT_scale=a_scales[:, g * B : (g + 1) * B],
                    rhs=codes[:, gl * ROWS : (gl + 1) * ROWS].bitcast(E5M2),
                    rhs_scale=scales[:, gl * ROWS : (gl + 1) * ROWS],
                    start=(not recurrent and g == 0),
                    stop=(recurrent == 1 and g == PASSES - 1),
                )

        def spread_bias(block, copy):
            bank = turn_psum.tile([P, 2 * ROWS], F32, name="spread", tag="turned")
            for gate in range(2):
                m = gate * BLOCKS + block
                nc.tensor.matmul(
                    bank[:, gate * ROWS : (gate + 1) * ROWS],
                    lhsT=pick[:, m : m + 1].to_broadcast([P, P]),
                    rhs=bias_rows[:],
                    start=True,
                    stop=True,
                )
            copy(out=bias[:, block, :], in_=bank[:])

        def turn_ig(pair):
            live["igT", pair] = acc_psum.tile([P, 4, P], BF16, name="ig_turned", tag="ig_turned")
            for j in range(4):
                nc.tensor.transpose(live["igT", pair][:, j, :], live["ig", pair][:, j * B : (j + 1) * B], ident16[:])

        def turn_h():
            words = h_raw[:].bitcast(F32)
            for half in range(2):
                bank = turn_psum.tile([P, 2, 2, P], F32, name="h_turned", tag="turned")
                for gl in range(2):
                    first = (2 * half + gl) * 2 * P
                    for u in range(2):
                        nc.tensor.transpose(bank[:, gl, u, :], words[:, first + u : first + 2 * P : 2], ident32[:])
                target = h_grouped[:, half * 8 * B : (half + 1) * 8 * B].bitcast(F32)
                nc.scalar.copy(
                    out=target.rearrange("p (g b u) -> p g b u", g=2, u=2), in_=bank[:].rearrange("p g u b -> p g b u")
                )

        def add_bias(block, gate):
            live["z", gate] = gate_pool.tile([P, ROWS], F32, name="z", tag="z")
            nc.vector.tensor_tensor(
                out=live["z", gate][:], in0=live["acc", gate][:], in1=bias[:, block, gate * ROWS : (gate + 1) * ROWS], op=ALU.add
            )

        def squash(source, target, func):
            live[target] = gate_pool.tile([P, ROWS], F32, name=target, tag=target)
            nc.scalar.activation(out=live[target][:], in_=live[source][:], func=func)

        def forget(block):
            pair, a = divmod(block, 2)
            live["kept"] = gate_pool.tile([P, ROWS], F32, name="kept", tag="kept")
            nc.vector.tensor_tensor(
                out=live["kept"][:], in0=live["f"][:], in1=live["c", pair][:, a * ROWS : (a + 1) * ROWS], op=ALU.mult
            )

        def update_cell(block):
            pair, a = divmod(block, 2)
            live["c_next"] = gate_pool.tile([P, ROWS], F32, name="c_next", tag="c_next")
            nc.vector.tensor_tensor(
                out=live["c_next"][:].rearrange("b (r j) -> b r j", j=4),
                in0=live["kept"][:].rearrange("b (r j) -> b r j", j=4),
                in1=live["igT", pair][:].rearrange("b j r -> b r j")[:, a * (ROWS // 4) : (a + 1) * (ROWS // 4), :],
                op=ALU.add,
            )

        def update_hidden():
            live["h_next"] = gate_pool.tile([P, ROWS], F32, name="h_next", tag="h_next")
            nc.vector.tensor_tensor(out=live["h_next"][:], in0=live["o"][:], in1=live["tanh_c"][:], op=ALU.mult)

        def store(name, out, block):
            nc.sync.dma_start(out=out[:, block * ROWS : (block + 1) * ROWS], in_=live[name][:])

        for n, b in enumerate((b_if, b_io, b_hf, b_ho)):
            nc.scalar.dma_start(
                out=bias_rows[n * BLOCKS : (n + 1) * BLOCKS, :], in_=b.rearrange("(r n) o -> r (n o)", r=BLOCKS)
            )
        load_weights(0)
        load_weights(1)
        nc.sync.dma_start(out=x_raw[:], in_=x.rearrange("(g p j) b -> p g (j b)", g=PASSES, j=4))
        load_weights(2)
        nc.sync.dma_start(out=h_raw[:], in_=h)
        load_weights(3)
        load_state(0)
        for s in range(4, LEAD):
            load_weights(s)
        make_identity(nc, ident32[:])
        make_identity(nc, ident16[:])
        nc.vector.memset(bias_rows[32:64, :], 0.0)
        nc.vector.memset(bias_rows[64:128, :], 0.0)
        nc.vector.tensor_tensor(
            out=pick[:], in0=ident16[:, 0 : 2 * BLOCKS], in1=ident16[:, 2 * BLOCKS : 4 * BLOCKS], op=ALU.add
        )

        for s in range(STEPS + 4):
            block, phase = divmod(s - 3, 4)
            ending = 0 <= block < BLOCKS
            if s + LEAD < STEPS:
                load_weights(s + LEAD)
            if s % 8 == 4 and s // 8 + 1 < BLOCKS // 2:
                load_state(s // 8 + 1)
            if ending and phase == 3:
                store("c_next", out_1, block)
            if block >= 1 and phase == 0:
                store("h_next", out_0, block - 1)

            if ending and phase == 1 and block % 2 == 0:
                turn_ig(block // 2)
            if s < STEPS:
                turn_weights(s)
            if s == 0:
                spread_bias(0, lambda out, in_: nc.scalar.activation(out=out, in_=in_, func=ACT.Copy))
            if s == 2:
                turn_h()

            if 1 <= s <= STEPS:
                quantise_weights(s - 1, 0)
            if ending and phase == 2:
                update_cell(block)
            if s + 1 < STEPS and direct_passes(s + 1) < PASSES:
                split_words(s + 1)
            if 1 <= s <= STEPS:
                quantise_weights(s - 1, 1)
            if s < STEPS and vector_helps(s):
                group_words(nc.vector.tensor_copy, s, PASSES - 1)
            if s == 0:
                nc.vector.tensor_copy(
                    out=x_grouped[:].rearrange("p (g b j) -> p g b j", g=PASSES, j=4),
                    in_=x_raw[:].rearrange("p g (j b) -> p g b j", j=4),
                )
            if s == 1:
                nc.vector.quantize_mx(out=x_codes[:].bitcast(E4M3), scales=x_scales[:], in_=x_grouped[:])
            if s == 2:
                nc.vector.quantize_mx(out=h_codes[:].bitcast(E4M3), scales=h_scales[:], in_=h_grouped[:])

            if ending and phase == 3 and block + 1 < BLOCKS:
                spread_bias(block + 1, nc.vector.tensor_copy)
            if 2 <= s < STEPS + 2:
                multiply(s - 2)

            if ending and phase == 0:
                add_bias(block, 0)
                squash(("z", 0), "f", ACT.Sigmoid)
            if ending and phase == 1:
                forget(block)
            if ending and phase == 2:
                add_bias(block, 1)
                squash("c_next", "tanh_c", ACT.Tanh)
                squash(("z", 1), "o", ACT.Sigmoid)
            if ending and phase == 3:
                update_hidden()
